import numpy as np
import ml_dtypes


def mxq(x, axis, fmt="e4m3"):
    dtype, down = {"e4m3": (ml_dtypes.float8_e4m3fn, 7), "e5m2": (ml_dtypes.float8_e5m2, 14)}[fmt]
    v = np.moveaxis(np.asarray(x, np.float32).astype(ml_dtypes.bfloat16).astype(np.float64), axis, -1)
    blocks = v.reshape(v.shape[:-1] + (-1, 32))
    amax = np.abs(blocks).max(-1, keepdims=True)
    byte = np.maximum(np.where(amax > 0, np.frexp(amax)[1] - 1 + 127, 0) - down, 1)
    scale = np.exp2(byte - 127.0)
    codes = (blocks / scale).astype(np.float32).astype(dtype).astype(np.float64)
    return np.moveaxis((codes * scale).reshape(v.shape), -1, axis)


WIDE = False


def mx_kscale(k):
    if not WIDE:
        return np.ones(k)
    levels = np.array([10, -10, 5, -5, 0])
    a = np.random.permutation(np.resize(levels, k // 512 * 4)).reshape(k // 512, 4)
    idx = np.arange(k)
    return np.exp2(a[idx // 512, idx % 128 // 32])


BF16 = ml_dtypes.bfloat16


def bf(x):
    return np.asarray(x, np.float32).astype(BF16)


def f64(x):
    return np.asarray(x).astype(np.float64)


B, N, F, U, S = 2, 512, 128, 128, 2
C = S * (F + U)


def sigmoid(v):
    return 1.0 / (1.0 + np.exp(-v))


def random_walk():
    a = np.random.uniform(size=(N, N))
    return a / a.sum(axis=1, keepdims=True) * np.sqrt(N)


def setup_inputs():
    s = mx_kscale(N)
    return {"r_prev": bf(sigmoid(np.random.standard_normal((B, U, N))) * np.random.standard_normal((B, U, N)) * s),
            "h_diff": bf(np.random.standard_normal((B, N, S * F))),
            "u": bf(sigmoid(np.random.standard_normal((B, N, U)))),
            "state": bf(np.random.standard_normal((B, U * N))),
            "support0": bf(random_walk() / s[None, :]),
            "support1": bf(random_walk() / s[None, :]),
            "c_kernel": bf(np.random.standard_normal((C, U)) / np.sqrt(C))}


def diffuse(xq, supq):
    return np.concatenate([(xq @ sq.T) for sq in supq], axis=1)


def reference(r_prev, h_diff, u, state, support0, support1, c_kernel):
    supq = (mxq(f64(support0), 1, "e4m3"), mxq(f64(support1), 1, "e4m3"))
    c_state = diffuse(mxq(f64(r_prev), 2, "e4m3"), supq).transpose(0, 2, 1)
    hc = np.concatenate([f64(h_diff), c_state], axis=-1)
    c = np.tanh(mxq(hc, 2, "e4m3") @ mxq(f64(c_kernel), 0, "e4m3"))
    prev_t = f64(state).reshape(B, U, N).transpose(0, 2, 1)
    ug = f64(u)
    z = ug * prev_t + (1.0 - ug) * c
    return z.reshape(B, U * N)

@@ -1,0 +1,179 @@
+from contextlib import ExitStack
+
+import concourse.mybir as mybir
+from concourse.masks import make_identity
+
+F32 = mybir.dt.float32
+BF16 = mybir.dt.bfloat16
+U32 = mybir.dt.uint32
+U8 = mybir.dt.uint8
+FP8X4 = mybir.dt.float8_e4m3fn_x4
+ACT = mybir.ActivationFunctionType
+ALU = mybir.AluOpType
+
+P = 128
+PACK = 4
+BATCH = 2
+NODES = 512
+UNITS = 128
+SUPPORTS = 2
+FEATURES = 256
+HALVES = 2
+PAIR = 2
+HALF_NODES = NODES // HALVES
+WORDS = NODES // 2
+
+FLOPS = 2 * BATCH * SUPPORTS * UNITS * NODES * NODES + 2 * BATCH * NODES * (FEATURES + SUPPORTS * UNITS) * UNITS
+
+
+def tile_gcrnncell_pb_s_kernel(tc, r_prev, h_diff, u, state, support0, support1, c_kernel, out):
+    nc = tc.nc
+    supports = (support0, support1)
+    with ExitStack() as ctx:
+        keep = ctx.enter_context(tc.tile_pool(name="keep", bufs=1))
+        flipped = ctx.enter_context(tc.psum_pool(name="flipped", bufs=3))
+        diffused = ctx.enter_context(tc.psum_pool(name="diffused", bufs=3))
+        summed = ctx.enter_context(tc.psum_pool(name="summed", bufs=2))
+
+        ident = keep.tile([P, P], F32)
+        make_identity(nc, ident[:])
+        warm = keep.tile([P, 1], F32)
+        nc.vector.memset(warm[:], 0.0)
+        nc.scalar.activation(out=warm[:], in_=warm[:], func=ACT.Tanh)
+
+        r_sb = keep.tile([P, BATCH * NODES], BF16)
+        nc.sync.dma_start(out=r_sb[:].rearrange("k (b n) -> k b n", b=BATCH), in_=r_prev.rearrange("b k n -> k b n"))
+        sup_sb = {}
+        for g in range(HALVES):
+            for i in range(SUPPORTS):
+                sup_sb[i, g] = keep.tile([P, PAIR * NODES], BF16, name="sup_sb_%d_%d" % (i, g))
+                nc.sync.dma_start(
+                    out=sup_sb[i, g][:],
+                    in_=supports[i].rearrange("(p g e) n -> g p (e n)", g=HALVES, e=PAIR)[g],
+                )
+        hd_sb = keep.tile([P, BATCH * NODES // P * FEATURES], BF16)
+        nc.sync.dma_start(
+            out=hd_sb[:].rearrange("p (b x) -> p b x", b=BATCH),
+            in_=h_diff.rearrange("b (p j) c -> p b (j c)", p=P),
+        )
+        ck_sb = keep.tile([P, PACK, UNITS], BF16)
+        nc.sync.dma_start(out=ck_sb[:, 0:2, :], in_=c_kernel[0:FEATURES, :].rearrange("(q s) k -> q s k", s=2))
+        nc.sync.dma_start(out=ck_sb[:, 2:4, :], in_=c_kernel[FEATURES:, :].rearrange("(i q) k -> q i k", q=P))
+        st_sb = keep.tile([P, BATCH * NODES], BF16)
+        nc.sync.dma_start(out=st_sb[:].rearrange("k (b n) -> k b n", b=BATCH), in_=state.rearrange("b (k n) -> k b n", n=NODES))
+        u_sb = keep.tile([P, BATCH, HALVES, PAIR * UNITS], BF16)
+        nc.sync.dma_start(
+            out=u_sb[:].rearrange("p b g x -> p b (g x)"),
+            in_=u.rearrange("b (p j) k -> p b (j k)", p=P),
+        )
+
+        def quantise_flipped(bank, name):
+            columns = bank.shape[2]
+            grouped = keep.tile([P, columns * PACK], BF16, name=name + "_grouped", align_bytes=64)
+            codes = keep.tile([P, columns], U32, name=name + "_codes", align_bytes=64)
+            scales = keep.tile([P, columns], U8, name=name + "_scales", align_bytes=64)
+            nc.scalar.copy(
+                out=grouped[:].bitcast(F32).rearrange("q (c h) -> q c h", h=2),
+                in_=bank.rearrange("q h c -> q c h"),
+            )
+            nc.vector.quantize_mx(out=codes[:].bitcast(FP8X4), scales=scales[:], in_=grouped[:])
+            return codes, scales
+
+        r_words = r_sb[:].bitcast(F32).rearrange("k (b w) -> k b w", b=BATCH)
+        r_bank = flipped.tile([P, 2, BATCH * UNITS], F32, tag="flipped")
+        for b in range(BATCH):
+            for h in range(2):
+                nc.tensor.transpose(r_bank[:, h, b * UNITS : (b + 1) * UNITS], r_words[:, b, h * P : (h + 1) * P], ident[:])
+        r_codes, r_scales = quantise_flipped(r_bank[:], "r")
+
+        planes = [keep.tile([P, HALVES, 2, HALF_NODES], F32, name="planes_%d" % b) for b in range(BATCH)]
+        for g in range(HALVES):
+            sup_q = []
+            for i in range(SUPPORTS):
+                sup_words = sup_sb[i, g][:].bitcast(F32).rearrange("p (e w) -> p e w", e=PAIR)
+                sup_bank = flipped.tile([P, 2, HALF_NODES], F32, tag="flipped")
+                for e in range(PAIR):
+                    for h in range(2):
+                        nc.tensor.transpose(sup_bank[:, h, e * P : (e + 1) * P], sup_words[:, e, h * P : (h + 1) * P], ident[:])
+                sup_q.append(quantise_flipped(sup_bank[:], "sup_%d_%d" % (i, g)))
+            for b in range(BATCH):
+                d_bank = diffused.tile([P, SUPPORTS, HALF_NODES], F32, tag="diffused")
+                for i in range(SUPPORTS):
+                    nc.tensor.matmul_mx(
+                        out=d_bank[:, i, :],
+                        lhsT=r_codes[:, b * UNITS : (b + 1) * UNITS].bitcast(FP8X4),
+                        lhsT_scale=r_scales[:, b * UNITS : (b + 1) * UNITS],
+                        rhs=sup_q[i][0][:].bitcast(FP8X4),
+                        rhs_scale=sup_q[i][1][:],
+                        start=True,
+                        stop=True,
+                    )
+                nc.scalar.copy(
+                    out=planes[b][:, g, 1, :].bitcast(BF16).rearrange("q (c i) -> q c i", i=SUPPORTS),
+                    in_=d_bank[:].rearrange("q i c -> q c i"),
+                )
+
+        ck_grouped = keep.tile([P, UNITS, PACK], BF16, align_bytes=64)
+        ck_codes = keep.tile([P, UNITS], U32, align_bytes=64)
+        ck_scales = keep.tile([P, UNITS], U8, align_bytes=64)
+        nc.vector.tensor_copy(out=ck_grouped[:], in_=ck_sb[:].rearrange("q t k -> q k t"))
+        nc.vector.quantize_mx(out=ck_codes[:].bitcast(FP8X4), scales=ck_scales[:], in_=ck_grouped[:].rearrange("q k t -> q (k t)"))
+
+        hd_words = hd_sb[:].bitcast(F32).rearrange("p (b j w) -> p b j w", b=BATCH, w=FEATURES // 2)
+        for b in range(BATCH):
+            h_bank = flipped.tile([P, HALVES, HALF_NODES], F32, tag="flipped")
+            for g in range(HALVES):
+                for e in range(PAIR):
+                    nc.tensor.transpose(h_bank[:, g, e * P : (e + 1) * P], hd_words[:, b, g * PAIR + e, :], ident[:])
+            nc.scalar.copy(out=planes[b][:, :, 0, :], in_=h_bank[:])
+
+        st_words = st_sb[:].bitcast(F32).rearrange("k (b p g) -> k b g p", b=BATCH, g=HALVES)
+        st_bank = flipped.tile([P, HALVES, BATCH, UNITS], F32, tag="flipped")
+        for g in range(HALVES):
+            for b in range(BATCH):
+                nc.tensor.transpose(st_bank[:, g, b, :], st_words[:, b, g, :], ident[:])
+        prev_t = st_bank[:].rearrange("p g b k -> p (g b k)").bitcast(BF16).rearrange(
+            "p (g b k e) -> p g b e k", g=HALVES, b=BATCH, e=PAIR
+        )
+        kept = keep.tile([P, HALVES, BATCH, PAIR, UNITS], F32)
+        for g in range(HALVES):
+            nc.vector.tensor_tensor(
+                out=kept[:, g],
+                in0=u_sb[:, :, g, :].rearrange("p b (e k) -> p b e k", e=PAIR),
+                in1=prev_t[:, g],
+                op=ALU.mult,
+            )
+
+        out_view = out.rearrange("b (p g x) -> g p b x", p=P, g=HALVES)
+        for g in range(HALVES):
+            c_bank = summed.tile([P, BATCH, PAIR, UNITS], F32, tag="summed")
+            for b in range(BATCH):
+                hc_grouped = keep.tile([P, HALF_NODES * PACK], BF16, name="hc_grouped_%d_%d" % (b, g), align_bytes=64)
+                hc_codes = keep.tile([P, HALF_NODES], U32, name="hc_codes_%d_%d" % (b, g), align_bytes=64)
+                hc_scales = keep.tile([P, HALF_NODES], U8, name="hc_scales_%d_%d" % (b, g), align_bytes=64)
+                nc.vector.tensor_copy(
+                    out=hc_grouped[:].bitcast(F32).rearrange("q (c w) -> q c w", w=2),
+                    in_=planes[b][:, g].rearrange("q w c -> q c w"),
+                )
+                nc.vector.quantize_mx(out=hc_codes[:].bitcast(FP8X4), scales=hc_scales[:], in_=hc_grouped[:])
+                for e in range(PAIR):
+                    nc.tensor.matmul_mx(
+                        out=c_bank[:, b, e, :],
+                        lhsT=hc_codes[:, e * P : (e + 1) * P].bitcast(FP8X4),
+                        lhsT_scale=hc_scales[:, e * P : (e + 1) * P],
+                        rhs=ck_codes[:].bitcast(FP8X4),
+                        rhs_scale=ck_scales[:],
+                        start=True,
+                        stop=True,
+                    )
+            cand = keep.tile([P, BATCH, PAIR * UNITS], F32, name="cand_%d" % g)
+            nc.scalar.activation(out=cand[:], in_=c_bank[:].rearrange("p b e k -> p b (e k)"), func=ACT.Tanh)
+            minus = keep.tile([P, BATCH, PAIR * UNITS], F32, name="minus_%d" % g)
+            nc.vector.scalar_tensor_tensor(
+                out=minus[:], in0=u_sb[:, :, g, :], scalar=1.0, in1=cand[:], op0=ALU.subtract, op1=ALU.mult
+            )
+            z = keep.tile([P, BATCH, PAIR * UNITS], F32, name="z_%d" % g)
+            nc.vector.tensor_tensor(
+                out=z[:], in0=kept[:, g].rearrange("p b e k -> p b (e k)"), in1=minus[:], op=ALU.subtract
+            )
+            nc.sync.dma_start(out=out_view[g], in_=z[:])

@@ -31,9 +31,8 @@ def tile_gcrnncell_pb_s_kernel(tc, r_prev, h_diff, u, state, support0, support1,
     supports = (support0, support1)
     with ExitStack() as ctx:
         keep = ctx.enter_context(tc.tile_pool(name="keep", bufs=1))
-        flipped = ctx.enter_context(tc.psum_pool(name="flipped", bufs=3))
-        diffused = ctx.enter_context(tc.psum_pool(name="diffused", bufs=3))
-        summed = ctx.enter_context(tc.psum_pool(name="summed", bufs=2))
+        banks = ctx.enter_context(tc.psum_pool(name="banks", bufs=8))
+        ctx.enter_context(tc.manual_schedule())
 
         ident = keep.tile([P, P], F32)
         make_identity(nc, ident[:])
@@ -51,14 +50,13 @@ def tile_gcrnncell_pb_s_kernel(tc, r_prev, h_diff, u, state, support0, support1,
                     out=sup_sb[i, g][:],
                     in_=supports[i].rearrange("(p g e) n -> g p (e n)", g=HALVES, e=PAIR)[g],
                 )
-        hd_sb = keep.tile([P, BATCH * NODES // P * FEATURES], BF16)
-        nc.sync.dma_start(
-            out=hd_sb[:].rearrange("p (b x) -> p b x", b=BATCH),
-            in_=h_diff.rearrange("b (p j) c -> p b (j c)", p=P),
-        )
         ck_sb = keep.tile([P, PACK, UNITS], BF16)
         nc.sync.dma_start(out=ck_sb[:, 0:2, :], in_=c_kernel[0:FEATURES, :].rearrange("(q s) k -> q s k", s=2))
         nc.sync.dma_start(out=ck_sb[:, 2:4, :], in_=c_kernel[FEATURES:, :].rearrange("(i q) k -> q i k", q=P))
+        hd_sb = []
+        for b in range(BATCH):
+            hd_sb.append(keep.tile([P, NODES // P * FEATURES], BF16, name="hd_sb_%d" % b))
+            nc.sync.dma_start(out=hd_sb[b][:], in_=h_diff[b].rearrange("(p j) c -> p (j c)", p=P))
         st_sb = keep.tile([P, BATCH * NODES], BF16)
         nc.sync.dma_start(out=st_sb[:].rearrange("k (b n) -> k b n", b=BATCH), in_=state.rearrange("b (k n) -> k b n", n=NODES))
         u_sb = keep.tile([P, BATCH, HALVES, PAIR * UNITS], BF16)
@@ -80,62 +78,112 @@ def tile_gcrnncell_pb_s_kernel(tc, r_prev, h_diff, u, state, support0, support1,
             return codes, scales
 
         r_words = r_sb[:].bitcast(F32).rearrange("k (b w) -> k b w", b=BATCH)
-        r_bank = flipped.tile([P, 2, BATCH * UNITS], F32, tag="flipped")
+        r_bank = banks.tile([P, 2, BATCH * UNITS], F32, tag="bank")
         for b in range(BATCH):
             for h in range(2):
                 nc.tensor.transpose(r_bank[:, h, b * UNITS : (b + 1) * UNITS], r_words[:, b, h * P : (h + 1) * P], ident[:])
         r_codes, r_scales = quantise_flipped(r_bank[:], "r")
+        sup_q = {}
 
-        planes = [keep.tile([P, HALVES, 2, HALF_NODES], F32, name="planes_%d" % b) for b in range(BATCH)]
-        for g in range(HALVES):
-            sup_q = []
-            for i in range(SUPPORTS):
-                sup_words = sup_sb[i, g][:].bitcast(F32).rearrange("p (e w) -> p e w", e=PAIR)
-                sup_bank = flipped.tile([P, 2, HALF_NODES], F32, tag="flipped")
-                for e in range(PAIR):
-                    for h in range(2):
-                        nc.tensor.transpose(sup_bank[:, h, e * P : (e + 1) * P], sup_words[:, e, h * P : (h + 1) * P], ident[:])
-                sup_q.append(quantise_flipped(sup_bank[:], "sup_%d_%d" % (i, g)))
-            for b in range(BATCH):
-                d_bank = diffused.tile([P, SUPPORTS, HALF_NODES], F32, tag="diffused")
-                for i in range(SUPPORTS):
-                    nc.tensor.matmul_mx(
-                        out=d_bank[:, i, :],
-                        lhsT=r_codes[:, b * UNITS : (b + 1) * UNITS].bitcast(FP8X4),
-                        lhsT_scale=r_scales[:, b * UNITS : (b + 1) * UNITS],
-                        rhs=sup_q[i][0][:].bitcast(FP8X4),
-                        rhs_scale=sup_q[i][1][:],
-                        start=True,
-                        stop=True,
-                    )
-                nc.scalar.copy(
-                    out=planes[b][:, g, 1, :].bitcast(BF16).rearrange("q (c i) -> q c i", i=SUPPORTS),
-                    in_=d_bank[:].rearrange("q i c -> q c i"),
-                )
+        def flip_support(i, g):
+            sup_words = sup_sb[i, g][:].bitcast(F32).rearrange("p (e w) -> p e w", e=PAIR)
+            sup_bank = banks.tile([P, 2, HALF_NODES], F32, tag="bank")
+            for e in range(PAIR):
+                for h in range(2):
+                    nc.tensor.transpose(sup_bank[:, h, e * P : (e + 1) * P], sup_words[:, e, h * P : (h + 1) * P], ident[:])
+            sup_q[i, g] = quantise_flipped(sup_bank[:], "sup_%d_%d" % (i, g))
+
 
         ck_grouped = keep.tile([P, UNITS, PACK], BF16, align_bytes=64)
         ck_codes = keep.tile([P, UNITS], U32, align_bytes=64)
         ck_scales = keep.tile([P, UNITS], U8, align_bytes=64)
+        flip_support(0, 0)
+        flip_support(1, 0)
         nc.vector.tensor_copy(out=ck_grouped[:], in_=ck_sb[:].rearrange("q t k -> q k t"))
+        flip_support(0, 1)
         nc.vector.quantize_mx(out=ck_codes[:].bitcast(FP8X4), scales=ck_scales[:], in_=ck_grouped[:].rearrange("q k t -> q (k t)"))
+        flip_support(1, 1)
 
-        hd_words = hd_sb[:].bitcast(F32).rearrange("p (b j w) -> p b j w", b=BATCH, w=FEATURES // 2)
+        planes = [keep.tile([P, HALVES, 2, HALF_NODES], F32, name="planes_%d" % b) for b in range(BATCH)]
+
+        def flip_h_diff(b):
+            hd_words = hd_sb[b][:].bitcast(F32).rearrange("p (j w) -> p j w", w=FEATURES // 2)
+            h_bank = banks.tile([P, HALVES, HALF_NODES], F32, tag="bank")
+            for j in range(HALVES * PAIR):
+                nc.tensor.transpose(h_bank[:, j // PAIR, (j % PAIR) * P : (j % PAIR + 1) * P], hd_words[:, j, :], ident[:])
+            nc.vector.tensor_copy(out=planes[b][:, :, 0, :], in_=h_bank[:])
+
+        def diffuse(b, g):
+            d_bank = banks.tile([P, SUPPORTS, HALF_NODES], F32, tag="bank")
+            for i in range(SUPPORTS):
+                nc.tensor.matmul_mx(
+                    out=d_bank[:, i, :],
+                    lhsT=r_codes[:, b * UNITS : (b + 1) * UNITS].bitcast(FP8X4),
+                    lhsT_scale=r_scales[:, b * UNITS : (b + 1) * UNITS],
+                    rhs=sup_q[i, g][0][:].bitcast(FP8X4),
+                    rhs_scale=sup_q[i, g][1][:],
+                    start=True,
+                    stop=True,
+                )
+            nc.scalar.copy(
+                out=planes[b][:, g, 1, :].bitcast(BF16).rearrange("q (c i) -> q c i", i=SUPPORTS),
+                in_=d_bank[:].rearrange("q i c -> q c i"),
+            )
+
+        c_bank = {}
+
+        hc_grouped = {}
+
+        def interleave(b, g):
+            hc_grouped[b, g] = keep.tile([P, HALF_NODES * PACK], BF16, name="hc_grouped_%d_%d" % (b, g), align_bytes=64)
+            nc.vector.tensor_copy(
+                out=hc_grouped[b, g][:].bitcast(F32).rearrange("q (c w) -> q c w", w=2),
+                in_=planes[b][:, g].rearrange("q w c -> q c w"),
+            )
+
+        def candidate_sums(b, g):
+            hc_codes = keep.tile([P, HALF_NODES], U32, name="hc_codes_%d_%d" % (b, g), align_bytes=64)
+            hc_scales = keep.tile([P, HALF_NODES], U8, name="hc_scales_%d_%d" % (b, g), align_bytes=64)
+            nc.vector.quantize_mx(out=hc_codes[:].bitcast(FP8X4), scales=hc_scales[:], in_=hc_grouped[b, g][:])
+            if b == 0:
+                c_bank[g] = banks.tile([P, BATCH, PAIR, UNITS], F32, tag="bank", name="c_bank_%d" % g)
+            for e in range(PAIR):
+                nc.tensor.matmul_mx(
+                    out=c_bank[g][:, b, e, :],
+                    lhsT=hc_codes[:, e * P : (e + 1) * P].bitcast(FP8X4),
+                    lhsT_scale=hc_scales[:, e * P : (e + 1) * P],
+                    rhs=ck_codes[:].bitcast(FP8X4),
+                    rhs_scale=ck_scales[:],
+                    start=True,
+                    stop=True,
+                )
+
+        kept = keep.tile([P, HALVES, BATCH, PAIR, UNITS], F32)
+        cand = [keep.tile([P, BATCH, PAIR * UNITS], F32, name="cand_%d" % g) for g in range(HALVES)]
+        out_view = out.rearrange("b (p g x) -> g p b x", p=P, g=HALVES)
+
+        minus = [keep.tile([P, BATCH, PAIR * UNITS], F32, name="minus_%d" % g) for g in range(HALVES)]
+
         for b in range(BATCH):
-            h_bank = flipped.tile([P, HALVES, HALF_NODES], F32, tag="flipped")
-            for g in range(HALVES):
-                for e in range(PAIR):
-                    nc.tensor.transpose(h_bank[:, g, e * P : (e + 1) * P], hd_words[:, b, g * PAIR + e, :], ident[:])
-            nc.scalar.copy(out=planes[b][:, :, 0, :], in_=h_bank[:])
-
+            flip_h_diff(b)
+        for b in range(BATCH):
+            diffuse(b, 0)
         st_words = st_sb[:].bitcast(F32).rearrange("k (b p g) -> k b g p", b=BATCH, g=HALVES)
-        st_bank = flipped.tile([P, HALVES, BATCH, UNITS], F32, tag="flipped")
+        st_bank = banks.tile([P, HALVES, BATCH, UNITS], F32, tag="bank")
         for g in range(HALVES):
             for b in range(BATCH):
                 nc.tensor.transpose(st_bank[:, g, b, :], st_words[:, b, g, :], ident[:])
         prev_t = st_bank[:].rearrange("p g b k -> p (g b k)").bitcast(BF16).rearrange(
             "p (g b k e) -> p g b e k", g=HALVES, b=BATCH, e=PAIR
         )
-        kept = keep.tile([P, HALVES, BATCH, PAIR, UNITS], F32)
+        for b in range(BATCH):
+            diffuse(b, 1)
+        for g in range(HALVES):
+            for b in range(BATCH):
+                interleave(b, g)
+            for b in range(BATCH):
+                candidate_sums(b, g)
+            nc.scalar.activation(out=cand[g][:], in_=c_bank[g][:].rearrange("p b e k -> p b (e k)"), func=ACT.Tanh)
         for g in range(HALVES):
             nc.vector.tensor_tensor(
                 out=kept[:, g],
@@ -143,37 +191,13 @@ def tile_gcrnncell_pb_s_kernel(tc, r_prev, h_diff, u, state, support0, support1,
                 in1=prev_t[:, g],
                 op=ALU.mult,
             )
-
-        out_view = out.rearrange("b (p g x) -> g p b x", p=P, g=HALVES)
         for g in range(HALVES):
-            c_bank = summed.tile([P, BATCH, PAIR, UNITS], F32, tag="summed")
-            for b in range(BATCH):
-                hc_grouped = keep.tile([P, HALF_NODES * PACK], BF16, name="hc_grouped_%d_%d" % (b, g), align_bytes=64)
-                hc_codes = keep.tile([P, HALF_NODES], U32, name="hc_codes_%d_%d" % (b, g), align_bytes=64)
-                hc_scales = keep.tile([P, HALF_NODES], U8, name="hc_scales_%d_%d" % (b, g), align_bytes=64)
-                nc.vector.tensor_copy(
-                    out=hc_grouped[:].bitcast(F32).rearrange("q (c w) -> q c w", w=2),
-                    in_=planes[b][:, g].rearrange("q w c -> q c w"),
-                )
-                nc.vector.quantize_mx(out=hc_codes[:].bitcast(FP8X4), scales=hc_scales[:], in_=hc_grouped[:])
-                for e in range(PAIR):
-                    nc.tensor.matmul_mx(
-                        out=c_bank[:, b, e, :],
-                        lhsT=hc_codes[:, e * P : (e + 1) * P].bitcast(FP8X4),
-                        lhsT_scale=hc_scales[:, e * P : (e + 1) * P],
-                        rhs=ck_codes[:].bitcast(FP8X4),
-                        rhs_scale=ck_scales[:],
-                        start=True,
-                        stop=True,
-                    )
-            cand = keep.tile([P, BATCH, PAIR * UNITS], F32, name="cand_%d" % g)
-            nc.scalar.activation(out=cand[:], in_=c_bank[:].rearrange("p b e k -> p b (e k)"), func=ACT.Tanh)
-            minus = keep.tile([P, BATCH, PAIR * UNITS], F32, name="minus_%d" % g)
             nc.vector.scalar_tensor_tensor(
-                out=minus[:], in0=u_sb[:, :, g, :], scalar=1.0, in1=cand[:], op0=ALU.subtract, op1=ALU.mult
+                out=minus[g][:], in0=u_sb[:, :, g, :], scalar=1.0, in1=cand[g][:], op0=ALU.subtract, op1=ALU.mult
             )
+        for g in range(HALVES):
             z = keep.tile([P, BATCH, PAIR * UNITS], F32, name="z_%d" % g)
             nc.vector.tensor_tensor(
-                out=z[:], in0=kept[:, g].rearrange("p b e k -> p b (e k)"), in1=minus[:], op=ALU.subtract
+                out=z[:], in0=kept[:, g].rearrange("p b e k -> p b (e k)"), in1=minus[g][:], op=ALU.subtract
             )
             nc.sync.dma_start(out=out_view[g], in_=z[:])

@@ -65,44 +65,34 @@ def tile_gcrnncell_pb_s_kernel(tc, r_prev, h_diff, u, state, support0, support1,
             in_=u.rearrange("b (p j) k -> p b (j k)", p=P),
         )
 
-        def quantise_flipped(bank, name):
-            columns = bank.shape[2]
-            grouped = keep.tile([P, columns * PACK], BF16, name=name + "_grouped", align_bytes=64)
-            codes = keep.tile([P, columns], U32, name=name + "_codes", align_bytes=64)
-            scales = keep.tile([P, columns], U8, name=name + "_scales", align_bytes=64)
-            nc.scalar.copy(
-                out=grouped[:].bitcast(F32).rearrange("q (c h) -> q c h", h=2),
-                in_=bank.rearrange("q h c -> q c h"),
-            )
-            nc.vector.quantize_mx(out=codes[:].bitcast(FP8X4), scales=scales[:], in_=grouped[:])
-            return codes, scales
+        def copy(second, g, out_ap, in_ap):
+            if second and g == 0:
+                nc.vector.tensor_copy(out=out_ap, in_=in_ap)
+            else:
+                nc.scalar.copy(out=out_ap, in_=in_ap)
 
-        r_words = r_sb[:].bitcast(F32).rearrange("k (b w) -> k b w", b=BATCH)
-        r_bank = banks.tile([P, 2, BATCH * UNITS], F32, tag="bank")
-        for b in range(BATCH):
-            for h in range(2):
-                nc.tensor.transpose(r_bank[:, h, b * UNITS : (b + 1) * UNITS], r_words[:, b, h * P : (h + 1) * P], ident[:])
-        r_codes, r_scales = quantise_flipped(r_bank[:], "r")
-        sup_q = {}
+        grouped = {}
+        codes = {}
+        scales = {}
+
+        def operand(name, columns):
+            grouped[name] = keep.tile([P, columns * PACK], BF16, name="grouped_%s" % name, align_bytes=64)
+            codes[name] = keep.tile([P, columns], U32, name="codes_%s" % name, align_bytes=64)
+            scales[name] = keep.tile([P, columns], U8, name="scales_%s" % name, align_bytes=64)
+
+        def quantise(name):
+            nc.vector.quantize_mx(out=codes[name][:].bitcast(FP8X4), scales=scales[name][:], in_=grouped[name][:])
+
+        def flip(name, rows, second, g):
+            operand(name, 2 * P)
+            bank = banks.tile([P, 2, 2 * P], F32, tag="bank", name="bank_%s" % name)
+            for block in range(2):
+                for h in range(2):
+                    nc.tensor.transpose(bank[:, h, block * P : (block + 1) * P], rows[:, block, h * P : (h + 1) * P], ident[:])
+            copy(second, g, grouped[name][:].bitcast(F32).rearrange("q (c h) -> q c h", h=2), bank[:].rearrange("q h c -> q c h"))
 
         def flip_support(i, g):
-            sup_words = sup_sb[i, g][:].bitcast(F32).rearrange("p (e w) -> p e w", e=PAIR)
-            sup_bank = banks.tile([P, 2, HALF_NODES], F32, tag="bank")
-            for e in range(PAIR):
-                for h in range(2):
-                    nc.tensor.transpose(sup_bank[:, h, e * P : (e + 1) * P], sup_words[:, e, h * P : (h + 1) * P], ident[:])
-            sup_q[i, g] = quantise_flipped(sup_bank[:], "sup_%d_%d" % (i, g))
-
-
-        ck_grouped = keep.tile([P, UNITS, PACK], BF16, align_bytes=64)
-        ck_codes = keep.tile([P, UNITS], U32, align_bytes=64)
-        ck_scales = keep.tile([P, UNITS], U8, align_bytes=64)
-        flip_support(0, 0)
-        flip_support(1, 0)
-        nc.vector.tensor_copy(out=ck_grouped[:], in_=ck_sb[:].rearrange("q t k -> q k t"))
-        flip_support(0, 1)
-        nc.vector.quantize_mx(out=ck_codes[:].bitcast(FP8X4), scales=ck_scales[:], in_=ck_grouped[:].rearrange("q k t -> q (k t)"))
-        flip_support(1, 1)
+            flip("sup_%d_%d" % (i, g), sup_sb[i, g][:].bitcast(F32).rearrange("p (e w) -> p e w", e=PAIR), i == 1, g)
 
         planes = [keep.tile([P, HALVES, 2, HALF_NODES], F32, name="planes_%d" % b) for b in range(BATCH)]
 
@@ -111,63 +101,89 @@ def tile_gcrnncell_pb_s_kernel(tc, r_prev, h_diff, u, state, support0, support1,
             h_bank = banks.tile([P, HALVES, HALF_NODES], F32, tag="bank")
             for j in range(HALVES * PAIR):
                 nc.tensor.transpose(h_bank[:, j // PAIR, (j % PAIR) * P : (j % PAIR + 1) * P], hd_words[:, j, :], ident[:])
-            nc.vector.tensor_copy(out=planes[b][:, :, 0, :], in_=h_bank[:])
+            copy(b == 1, 0, planes[b][:, :, 0, :], h_bank[:])
 
         def diffuse(b, g):
             d_bank = banks.tile([P, SUPPORTS, HALF_NODES], F32, tag="bank")
             for i in range(SUPPORTS):
                 nc.tensor.matmul_mx(
                     out=d_bank[:, i, :],
-                    lhsT=r_codes[:, b * UNITS : (b + 1) * UNITS].bitcast(FP8X4),
-                    lhsT_scale=r_scales[:, b * UNITS : (b + 1) * UNITS],
-                    rhs=sup_q[i, g][0][:].bitcast(FP8X4),
-                    rhs_scale=sup_q[i, g][1][:],
+                    lhsT=codes["r"][:, b * UNITS : (b + 1) * UNITS].bitcast(FP8X4),
+                    lhsT_scale=scales["r"][:, b * UNITS : (b + 1) * UNITS],
+                    rhs=codes["sup_%d_%d" % (i, g)][:].bitcast(FP8X4),
+                    rhs_scale=scales["sup_%d_%d" % (i, g)][:],
                     start=True,
                     stop=True,
                 )
-            nc.scalar.copy(
-                out=planes[b][:, g, 1, :].bitcast(BF16).rearrange("q (c i) -> q c i", i=SUPPORTS),
-                in_=d_bank[:].rearrange("q i c -> q c i"),
+            copy(
+                b == 1,
+                g,
+                planes[b][:, g, 1, :].bitcast(BF16).rearrange("q (c i) -> q c i", i=SUPPORTS),
+                d_bank[:].rearrange("q i c -> q c i"),
+            )
+
+        def interleave(b, g):
+            operand("hc_%d_%d" % (b, g), HALF_NODES)
+            copy(
+                True,
+                g,
+                grouped["hc_%d_%d" % (b, g)][:].bitcast(F32).rearrange("q (c w) -> q c w", w=2),
+                planes[b][:, g].rearrange("q w c -> q c w"),
             )
 
         c_bank = {}
 
-        hc_grouped = {}
-
-        def interleave(b, g):
-            hc_grouped[b, g] = keep.tile([P, HALF_NODES * PACK], BF16, name="hc_grouped_%d_%d" % (b, g), align_bytes=64)
-            nc.vector.tensor_copy(
-                out=hc_grouped[b, g][:].bitcast(F32).rearrange("q (c w) -> q c w", w=2),
-                in_=planes[b][:, g].rearrange("q w c -> q c w"),
-            )
-
         def candidate_sums(b, g):
-            hc_codes = keep.tile([P, HALF_NODES], U32, name="hc_codes_%d_%d" % (b, g), align_bytes=64)
-            hc_scales = keep.tile([P, HALF_NODES], U8, name="hc_scales_%d_%d" % (b, g), align_bytes=64)
-            nc.vector.quantize_mx(out=hc_codes[:].bitcast(FP8X4), scales=hc_scales[:], in_=hc_grouped[b, g][:])
-            if b == 0:
-                c_bank[g] = banks.tile([P, BATCH, PAIR, UNITS], F32, tag="bank", name="c_bank_%d" % g)
+            name = "hc_%d_%d" % (b, g)
+            quantise(name)
+            c_bank[b, g] = banks.tile([P, PAIR * UNITS], F32, tag="bank", name="c_bank_%d_%d" % (b, g))
             for e in range(PAIR):
                 nc.tensor.matmul_mx(
-                    out=c_bank[g][:, b, e, :],
-                    lhsT=hc_codes[:, e * P : (e + 1) * P].bitcast(FP8X4),
-                    lhsT_scale=hc_scales[:, e * P : (e + 1) * P],
-                    rhs=ck_codes[:].bitcast(FP8X4),
-                    rhs_scale=ck_scales[:],
+                    out=c_bank[b, g][:, e * UNITS : (e + 1) * UNITS],
+                    lhsT=codes[name][:, e * P : (e + 1) * P].bitcast(FP8X4),
+                    lhsT_scale=scales[name][:, e * P : (e + 1) * P],
+                    rhs=codes["ck"][:].bitcast(FP8X4),
+                    rhs_scale=scales["ck"][:],
                     start=True,
                     stop=True,
                 )
 
         kept = keep.tile([P, HALVES, BATCH, PAIR, UNITS], F32)
-        cand = [keep.tile([P, BATCH, PAIR * UNITS], F32, name="cand_%d" % g) for g in range(HALVES)]
-        out_view = out.rearrange("b (p g x) -> g p b x", p=P, g=HALVES)
+        out_view = out.rearrange("b (p g x) -> b g p x", p=P, g=HALVES)
 
-        minus = [keep.tile([P, BATCH, PAIR * UNITS], F32, name="minus_%d" % g) for g in range(HALVES)]
+        def blend(g):
+            cand = [keep.tile([P, PAIR * UNITS], F32, name="cand_%d_%d" % (b, g)) for b in range(BATCH)]
+            minus = [keep.tile([P, PAIR * UNITS], F32, name="minus_%d_%d" % (b, g)) for b in range(BATCH)]
+            z = [keep.tile([P, PAIR * UNITS], F32, name="z_%d_%d" % (b, g)) for b in range(BATCH)]
+            for b in range(BATCH):
+                nc.scalar.activation(out=cand[b][:], in_=c_bank[b, g][:], func=ACT.Tanh)
+            for b in range(BATCH):
+                nc.vector.scalar_tensor_tensor(
+                    out=minus[b][:], in0=u_sb[:, b, g, :], scalar=1.0, in1=cand[b][:], op0=ALU.subtract, op1=ALU.mult
+                )
+            for b in range(BATCH):
+                nc.vector.tensor_tensor(
+                    out=z[b][:], in0=kept[:, g, b].rearrange("p e k -> p (e k)"), in1=minus[b][:], op=ALU.subtract
+                )
+                nc.sync.dma_start(out=out_view[b, g], in_=z[b][:])
 
+        flip("r", r_sb[:].bitcast(F32).rearrange("k (b w) -> k b w", b=BATCH), False, 0)
+        quantise("r")
+        flip_support(0, 0)
+        flip_support(1, 0)
+        operand("ck", UNITS)
+        nc.vector.tensor_copy(out=grouped["ck"][:].rearrange("q (k t) -> q k t", t=PACK), in_=ck_sb[:].rearrange("q t k -> q k t"))
+        quantise("sup_0_0")
+        quantise("sup_1_0")
+        for i in range(SUPPORTS):
+            flip_support(i, 1)
+            quantise("sup_%d_1" % i)
         for b in range(BATCH):
             flip_h_diff(b)
-        for b in range(BATCH):
-            diffuse(b, 0)
+        quantise("ck")
+        for g in range(HALVES):
+            for b in range(BATCH):
+                diffuse(b, g)
         st_words = st_sb[:].bitcast(F32).rearrange("k (b p g) -> k b g p", b=BATCH, g=HALVES)
         st_bank = banks.tile([P, HALVES, BATCH, UNITS], F32, tag="bank")
         for g in range(HALVES):
@@ -177,13 +193,11 @@ def tile_gcrnncell_pb_s_kernel(tc, r_prev, h_diff, u, state, support0, support1,
             "p (g b k e) -> p g b e k", g=HALVES, b=BATCH, e=PAIR
         )
         for b in range(BATCH):
-            diffuse(b, 1)
-        for g in range(HALVES):
-            for b in range(BATCH):
-                interleave(b, g)
-            for b in range(BATCH):
-                candidate_sums(b, g)
-            nc.scalar.activation(out=cand[g][:], in_=c_bank[g][:].rearrange("p b e k -> p b (e k)"), func=ACT.Tanh)
+            interleave(b, 0)
+        for b in range(BATCH):
+            candidate_sums(b, 0)
+        for b in range(BATCH):
+            interleave(b, 1)
         for g in range(HALVES):
             nc.vector.tensor_tensor(
                 out=kept[:, g],
@@ -191,13 +205,7 @@ def tile_gcrnncell_pb_s_kernel(tc, r_prev, h_diff, u, state, support0, support1,
                 in1=prev_t[:, g],
                 op=ALU.mult,
             )
+        for b in range(BATCH):
+            candidate_sums(b, 1)
         for g in range(HALVES):
-            nc.vector.scalar_tensor_tensor(
-                out=minus[g][:], in0=u_sb[:, :, g, :], scalar=1.0, in1=cand[g][:], op0=ALU.subtract, op1=ALU.mult
-            )
-        for g in range(HALVES):
-            z = keep.tile([P, BATCH, PAIR * UNITS], F32, name="z_%d" % g)
-            nc.vector.tensor_tensor(
-                out=z[:], in0=kept[:, g].rearrange("p b e k -> p b (e k)"), in1=minus[g][:], op=ALU.subtract
-            )
-            nc.sync.dma_start(out=out_view[g], in_=z[:])
+            blend(g)

@@ -32,7 +32,6 @@ def tile_gcrnncell_pb_s_kernel(tc, r_prev, h_diff, u, state, support0, support1,
     with ExitStack() as ctx:
         keep = ctx.enter_context(tc.tile_pool(name="keep", bufs=1))
         banks = ctx.enter_context(tc.psum_pool(name="banks", bufs=8))
-        ctx.enter_context(tc.manual_schedule())
 
         ident = keep.tile([P, P], F32)
         make_identity(nc, ident[:])

@@ -7,6 +7,7 @@ F32 = mybir.dt.float32
 BF16 = mybir.dt.bfloat16
 U32 = mybir.dt.uint32
 U8 = mybir.dt.uint8
+I32 = mybir.dt.int32
 FP8X4 = mybir.dt.float8_e4m3fn_x4
 ACT = mybir.ActivationFunctionType
 ALU = mybir.AluOpType
@@ -23,6 +24,8 @@ PAIR = 2
 HALF_NODES = NODES // HALVES
 WORDS = NODES // 2
 
+WARM_PASSES = 9
+
 FLOPS = 2 * BATCH * SUPPORTS * UNITS * NODES * NODES + 2 * BATCH * NODES * (FEATURES + SUPPORTS * UNITS) * UNITS
 
 
@@ -32,12 +35,30 @@ def tile_gcrnncell_pb_s_kernel(tc, r_prev, h_diff, u, state, support0, support1,
     with ExitStack() as ctx:
         keep = ctx.enter_context(tc.tile_pool(name="keep", bufs=1))
         banks = ctx.enter_context(tc.psum_pool(name="banks", bufs=8))
+        ctx.enter_context(tc.manual_schedule())
 
         ident = keep.tile([P, P], F32)
         make_identity(nc, ident[:])
         warm = keep.tile([P, 1], F32)
         nc.vector.memset(warm[:], 0.0)
         nc.scalar.activation(out=warm[:], in_=warm[:], func=ACT.Tanh)
+
+        idle_values = keep.tile([P, HALF_NODES * PACK], BF16, align_bytes=64)
+        idle_codes = keep.tile([P, HALF_NODES], U32, align_bytes=64)
+        idle_scales = keep.tile([P, HALF_NODES], U8, align_bytes=64)
+        nc.vector.memset(idle_values[:].bitcast(I32), 0)
+        nc.vector.quantize_mx(out=idle_codes[:].bitcast(FP8X4), scales=idle_scales[:], in_=idle_values[:])
+        idle_bank = banks.tile([P, HALF_NODES], F32, tag="bank")
+        for k in range(WARM_PASSES):
+            nc.tensor.matmul_mx(
+                out=idle_bank[:],
+                lhsT=idle_codes[:, 0:P].bitcast(FP8X4),
+                lhsT_scale=idle_scales[:, 0:P],
+                rhs=idle_codes[:].bitcast(FP8X4),
+                rhs_scale=idle_scales[:],
+                start=True,
+                stop=True,
+            )
 
         r_sb = keep.tile([P, BATCH * NODES], BF16)
         nc.sync.dma_start(out=r_sb[:].rearrange("k (b n) -> k b n", b=BATCH), in_=r_prev.rearrange("b k n -> k b n"))

@@ -70,13 +70,13 @@ def tile_gcrnncell_pb_s_kernel(tc, r_prev, h_diff, u, state, support0, support1,
                     out=sup_sb[i, g][:],
                     in_=supports[i].rearrange("(p g e) n -> g p (e n)", g=HALVES, e=PAIR)[g],
                 )
-        ck_sb = keep.tile([P, PACK, UNITS], BF16)
-        nc.sync.dma_start(out=ck_sb[:, 0:2, :], in_=c_kernel[0:FEATURES, :].rearrange("(q s) k -> q s k", s=2))
-        nc.sync.dma_start(out=ck_sb[:, 2:4, :], in_=c_kernel[FEATURES:, :].rearrange("(i q) k -> q i k", q=P))
         hd_sb = []
         for b in range(BATCH):
             hd_sb.append(keep.tile([P, NODES // P * FEATURES], BF16, name="hd_sb_%d" % b))
             nc.sync.dma_start(out=hd_sb[b][:], in_=h_diff[b].rearrange("(p j) c -> p (j c)", p=P))
+        ck_sb = keep.tile([P, PACK, UNITS], BF16)
+        nc.sync.dma_start(out=ck_sb[:, 0:2, :], in_=c_kernel[0:FEATURES, :].rearrange("(q s) k -> q s k", s=2))
+        nc.sync.dma_start(out=ck_sb[:, 2:4, :], in_=c_kernel[FEATURES:, :].rearrange("(i q) k -> q i k", q=P))
         st_sb = keep.tile([P, BATCH * NODES], BF16)
         nc.sync.dma_start(out=st_sb[:].rearrange("k (b n) -> k b n", b=BATCH), in_=state.rearrange("b (k n) -> k b n", n=NODES))
         u_sb = keep.tile([P, BATCH, HALVES, PAIR * UNITS], BF16)
@@ -85,8 +85,8 @@ def tile_gcrnncell_pb_s_kernel(tc, r_prev, h_diff, u, state, support0, support1,
             in_=u.rearrange("b (p j) k -> p b (j k)", p=P),
         )
 
-        def copy(second, g, out_ap, in_ap):
-            if second and g == 0:
+        def copy(engine, out_ap, in_ap):
+            if engine == "vector":
                 nc.vector.tensor_copy(out=out_ap, in_=in_ap)
             else:
                 nc.scalar.copy(out=out_ap, in_=in_ap)
@@ -103,16 +103,16 @@ def tile_gcrnncell_pb_s_kernel(tc, r_prev, h_diff, u, state, support0, support1,
         def quantise(name):
             nc.vector.quantize_mx(out=codes[name][:].bitcast(FP8X4), scales=scales[name][:], in_=grouped[name][:])
 
-        def flip(name, rows, second, g):
+        def flip(name, rows):
             operand(name, 2 * P)
             bank = banks.tile([P, 2, 2 * P], F32, tag="bank", name="bank_%s" % name)
             for block in range(2):
                 for h in range(2):
                     nc.tensor.transpose(bank[:, h, block * P : (block + 1) * P], rows[:, block, h * P : (h + 1) * P], ident[:])
-            copy(second, g, grouped[name][:].bitcast(F32).rearrange("q (c h) -> q c h", h=2), bank[:].rearrange("q h c -> q c h"))
+            copy("scalar", grouped[name][:].bitcast(F32).rearrange("q (c h) -> q c h", h=2), bank[:].rearrange("q h c -> q c h"))
 
         def flip_support(i, g):
-            flip("sup_%d_%d" % (i, g), sup_sb[i, g][:].bitcast(F32).rearrange("p (e w) -> p e w", e=PAIR), i == 1, g)
+            flip("sup_%d_%d" % (i, g), sup_sb[i, g][:].bitcast(F32).rearrange("p (e w) -> p e w", e=PAIR))
 
         planes = [keep.tile([P, HALVES, 2, HALF_NODES], F32, name="planes_%d" % b) for b in range(BATCH)]
 
@@ -121,7 +121,7 @@ def tile_gcrnncell_pb_s_kernel(tc, r_prev, h_diff, u, state, support0, support1,
             h_bank = banks.tile([P, HALVES, HALF_NODES], F32, tag="bank")
             for j in range(HALVES * PAIR):
                 nc.tensor.transpose(h_bank[:, j // PAIR, (j % PAIR) * P : (j % PAIR + 1) * P], hd_words[:, j, :], ident[:])
-            copy(b == 1, 0, planes[b][:, :, 0, :], h_bank[:])
+            copy(("scalar", "vector")[b], planes[b][:, :, 0, :], h_bank[:])
 
         def diffuse(b, g):
             d_bank = banks.tile([P, SUPPORTS, HALF_NODES], F32, tag="bank")
@@ -136,8 +136,7 @@ def tile_gcrnncell_pb_s_kernel(tc, r_prev, h_diff, u, state, support0, support1,
                     stop=True,
                 )
             copy(
-                b == 1,
-                g,
+                "scalar",
                 planes[b][:, g, 1, :].bitcast(BF16).rearrange("q (c i) -> q c i", i=SUPPORTS),
                 d_bank[:].rearrange("q i c -> q c i"),
             )
@@ -145,8 +144,7 @@ def tile_gcrnncell_pb_s_kernel(tc, r_prev, h_diff, u, state, support0, support1,
         def interleave(b, g):
             operand("hc_%d_%d" % (b, g), HALF_NODES)
             copy(
-                True,
-                g,
+                ("vector", "scalar")[g],
                 grouped["hc_%d_%d" % (b, g)][:].bitcast(F32).rearrange("q (c w) -> q c w", w=2),
                 planes[b][:, g].rearrange("q w c -> q c w"),
             )
@@ -187,23 +185,22 @@ def tile_gcrnncell_pb_s_kernel(tc, r_prev, h_diff, u, state, support0, support1,
                 )
                 nc.sync.dma_start(out=out_view[b, g], in_=z[b][:])
 
-        flip("r", r_sb[:].bitcast(F32).rearrange("k (b w) -> k b w", b=BATCH), False, 0)
+        flip("r", r_sb[:].bitcast(F32).rearrange("k (b w) -> k b w", b=BATCH))
         quantise("r")
-        flip_support(0, 0)
-        flip_support(1, 0)
+        for g in range(HALVES):
+            for i in range(SUPPORTS):
+                flip_support(i, g)
+                quantise("sup_%d_%d" % (i, g))
         operand("ck", UNITS)
         nc.vector.tensor_copy(out=grouped["ck"][:].rearrange("q (k t) -> q k t", t=PACK), in_=ck_sb[:].rearrange("q t k -> q k t"))
-        quantise("sup_0_0")
-        quantise("sup_1_0")
-        for i in range(SUPPORTS):
-            flip_support(i, 1)
-            quantise("sup_%d_1" % i)
         for b in range(BATCH):
             flip_h_diff(b)
+            diffuse(b, 0)
+        interleave(0, 0)
         quantise("ck")
-        for g in range(HALVES):
-            for b in range(BATCH):
-                diffuse(b, g)
+        interleave(1, 0)
+        for b in range(BATCH):
+            diffuse(b, 1)
         st_words = st_sb[:].bitcast(F32).rearrange("k (b p g) -> k b g p", b=BATCH, g=HALVES)
         st_bank = banks.tile([P, HALVES, BATCH, UNITS], F32, tag="bank")
         for g in range(HALVES):
@@ -212,8 +209,6 @@ def tile_gcrnncell_pb_s_kernel(tc, r_prev, h_diff, u, state, support0, support1,
         prev_t = st_bank[:].rearrange("p g b k -> p (g b k)").bitcast(BF16).rearrange(
             "p (g b k e) -> p g b e k", g=HALVES, b=BATCH, e=PAIR
         )
-        for b in range(BATCH):
-            interleave(b, 0)
         for b in range(BATCH):
             candidate_sums(b, 0)
         for b in range(BATCH):

@@ -39,6 +39,8 @@ def tile_gcrnncell_pb_s_kernel(tc, r_prev, h_diff, u, state, support0, support1,
 
         ident = keep.tile([P, P], F32)
         make_identity(nc, ident[:])
+        ident_bf = keep.tile([P, P], BF16)
+        make_identity(nc, ident_bf[:])
         warm = keep.tile([P, 1], F32)
         nc.vector.memset(warm[:], 0.0)
         nc.scalar.activation(out=warm[:], in_=warm[:], func=ACT.Tanh)
@@ -100,71 +102,102 @@ def tile_gcrnncell_pb_s_kernel(tc, r_prev, h_diff, u, state, support0, support1,
             codes[name] = keep.tile([P, columns], U32, name="codes_%s" % name, align_bytes=64)
             scales[name] = keep.tile([P, columns], U8, name="scales_%s" % name, align_bytes=64)
 
-        def quantise(name):
-            nc.vector.quantize_mx(out=codes[name][:].bitcast(FP8X4), scales=scales[name][:], in_=grouped[name][:])
+        def quantise(name, columns=slice(0, 2 * P)):
+            values = slice(columns.start * PACK, columns.stop * PACK)
+            nc.vector.quantize_mx(
+                out=codes[name][:, columns].bitcast(FP8X4), scales=scales[name][:, columns], in_=grouped[name][:, values]
+            )
 
-        def flip(name, rows):
+        def flip(name, rows, engine):
             operand(name, 2 * P)
             bank = banks.tile([P, 2, 2 * P], F32, tag="bank", name="bank_%s" % name)
             for block in range(2):
                 for h in range(2):
                     nc.tensor.transpose(bank[:, h, block * P : (block + 1) * P], rows[:, block, h * P : (h + 1) * P], ident[:])
-            copy("scalar", grouped[name][:].bitcast(F32).rearrange("q (c h) -> q c h", h=2), bank[:].rearrange("q h c -> q c h"))
+            copy(engine, grouped[name][:].bitcast(F32).rearrange("q (c h) -> q c h", h=2), bank[:].rearrange("q h c -> q c h"))
 
-        def flip_support(i, g):
-            flip("sup_%d_%d" % (i, g), sup_sb[i, g][:].bitcast(F32).rearrange("p (e w) -> p e w", e=PAIR))
+        def flip_support(i, g, engine):
+            flip("sup_%d_%d" % (i, g), sup_sb[i, g][:].bitcast(F32).rearrange("p (e w) -> p e w", e=PAIR), engine)
 
-        planes = [keep.tile([P, HALVES, 2, HALF_NODES], F32, name="planes_%d" % b) for b in range(BATCH)]
+        planes = [keep.tile([P, 2, HALF_NODES], F32, name="planes_%d" % b) for b in range(BATCH)]
 
         def flip_h_diff(b):
             hd_words = hd_sb[b][:].bitcast(F32).rearrange("p (j w) -> p j w", w=FEATURES // 2)
-            h_bank = banks.tile([P, HALVES, HALF_NODES], F32, tag="bank")
-            for j in range(HALVES * PAIR):
-                nc.tensor.transpose(h_bank[:, j // PAIR, (j % PAIR) * P : (j % PAIR + 1) * P], hd_words[:, j, :], ident[:])
-            copy(("scalar", "vector")[b], planes[b][:, :, 0, :], h_bank[:])
+            h_bank = banks.tile([P, HALF_NODES], F32, tag="bank")
+            for j in range(PAIR):
+                nc.tensor.transpose(h_bank[:, j * P : (j + 1) * P], hd_words[:, j, :], ident[:])
+            copy(("scalar", "vector")[b], planes[b][:, 0, :], h_bank[:])
 
-        def diffuse(b, g):
+        def diffuse(b):
             d_bank = banks.tile([P, SUPPORTS, HALF_NODES], F32, tag="bank")
             for i in range(SUPPORTS):
                 nc.tensor.matmul_mx(
                     out=d_bank[:, i, :],
                     lhsT=codes["r"][:, b * UNITS : (b + 1) * UNITS].bitcast(FP8X4),
                     lhsT_scale=scales["r"][:, b * UNITS : (b + 1) * UNITS],
-                    rhs=codes["sup_%d_%d" % (i, g)][:].bitcast(FP8X4),
-                    rhs_scale=scales["sup_%d_%d" % (i, g)][:],
+                    rhs=codes["sup_%d_0" % i][:].bitcast(FP8X4),
+                    rhs_scale=scales["sup_%d_0" % i][:],
                     start=True,
                     stop=True,
                 )
             copy(
                 "scalar",
-                planes[b][:, g, 1, :].bitcast(BF16).rearrange("q (c i) -> q c i", i=SUPPORTS),
+                planes[b][:, 1, :].bitcast(BF16).rearrange("q (c i) -> q c i", i=SUPPORTS),
                 d_bank[:].rearrange("q i c -> q c i"),
             )
 
-        def interleave(b, g):
-            operand("hc_%d_%d" % (b, g), HALF_NODES)
+        def interleave(b):
+            name = "hc_%d_0" % b
+            operand(name, HALF_NODES)
+            nc.vector.tensor_copy(
+                out=grouped[name][:].bitcast(F32).rearrange("q (c w) -> q c w", w=2),
+                in_=planes[b][:].rearrange("q w c -> q c w"),
+            )
+
+        hc_bank = {}
+
+        def bring_h_diff(b, e):
+            hc_bank[b, e] = banks.tile([P, PACK, P], F32, tag="bank", name="hc_bank_%d_%d" % (b, e))
+            first = (PAIR + e) * FEATURES
+            for s in range(2):
+                nc.tensor.matmul(
+                    out=hc_bank[b, e][:, s, :], lhsT=hd_sb[b][:, first + s : first + FEATURES : 2], rhs=ident_bf[:], start=True, stop=True
+                )
+
+        def diffuse_beside(b, e):
+            for i in range(SUPPORTS):
+                name = "sup_%d_1" % i
+                nc.tensor.matmul_mx(
+                    out=hc_bank[b, e][:, SUPPORTS + i, :],
+                    lhsT=codes["r"][:, b * UNITS : (b + 1) * UNITS].bitcast(FP8X4),
+                    lhsT_scale=scales["r"][:, b * UNITS : (b + 1) * UNITS],
+                    rhs=codes[name][:, e * P : (e + 1) * P].bitcast(FP8X4),
+                    rhs_scale=scales[name][:, e * P : (e + 1) * P],
+                    start=True,
+                    stop=True,
+                )
             copy(
-                ("vector", "scalar")[g],
-                grouped["hc_%d_%d" % (b, g)][:].bitcast(F32).rearrange("q (c w) -> q c w", w=2),
-                planes[b][:, g].rearrange("q w c -> q c w"),
+                "scalar",
+                grouped["hc_%d_1" % b][:, e * P * PACK : (e + 1) * P * PACK].rearrange("q (c t) -> q c t", t=PACK),
+                hc_bank[b, e][:].rearrange("q t c -> q c t"),
             )
 
         c_bank = {}
 
-        def candidate_sums(b, g):
-            name = "hc_%d_%d" % (b, g)
-            quantise(name)
+        def candidate_bank(b, g):
             c_bank[b, g] = banks.tile([P, PAIR * UNITS], F32, tag="bank", name="c_bank_%d_%d" % (b, g))
-            for e in range(PAIR):
-                nc.tensor.matmul_mx(
-                    out=c_bank[b, g][:, e * UNITS : (e + 1) * UNITS],
-                    lhsT=codes[name][:, e * P : (e + 1) * P].bitcast(FP8X4),
-                    lhsT_scale=scales[name][:, e * P : (e + 1) * P],
-                    rhs=codes["ck"][:].bitcast(FP8X4),
-                    rhs_scale=scales["ck"][:],
-                    start=True,
-                    stop=True,
-                )
+
+        def candidate_sums(b, g, e):
+            name = "hc_%d_%d" % (b, g)
+            nc.tensor.matmul_mx(
+                out=c_bank[b, g][:, e * UNITS : (e + 1) * UNITS],
+                lhsT=codes[name][:, e * P : (e + 1) * P].bitcast(FP8X4),
+                lhsT_scale=scales[name][:, e * P : (e + 1) * P],
+                rhs=codes["ck"][:].bitcast(FP8X4),
+                rhs_scale=scales["ck"][:],
+                start=True,
+                stop=True,
+            )
 
         kept = keep.tile([P, HALVES, BATCH, PAIR, UNITS], F32)
         out_view = out.rearrange("b (p g x) -> b g p x", p=P, g=HALVES)
@@ -185,22 +218,30 @@ def tile_gcrnncell_pb_s_kernel(tc, r_prev, h_diff, u, state, support0, support1,
                 )
                 nc.sync.dma_start(out=out_view[b, g], in_=z[b][:])
 
-        flip("r", r_sb[:].bitcast(F32).rearrange("k (b w) -> k b w", b=BATCH))
+        flip("r", r_sb[:].bitcast(F32).rearrange("k (b w) -> k b w", b=BATCH), "scalar")
+        flip_support(0, 0, "vector")
         quantise("r")
-        for g in range(HALVES):
-            for i in range(SUPPORTS):
-                flip_support(i, g)
-                quantise("sup_%d_%d" % (i, g))
+        quantise("sup_0_0")
+        flip_support(1, 0, "scalar")
+        quantise("sup_1_0")
+        for i in range(SUPPORTS):
+            flip_support(i, 1, "scalar")
+            quantise("sup_%d_1" % i)
         operand("ck", UNITS)
         nc.vector.tensor_copy(out=grouped["ck"][:].rearrange("q (k t) -> q k t", t=PACK), in_=ck_sb[:].rearrange("q t k -> q k t"))
         for b in range(BATCH):
             flip_h_diff(b)
-            diffuse(b, 0)
-        interleave(0, 0)
-        quantise("ck")
-        interleave(1, 0)
+            diffuse(b)
+        interleave(0)
+        quantise("ck", slice(0, UNITS))
+        interleave(1)
         for b in range(BATCH):
-            diffuse(b, 1)
+            for e in range(PAIR):
+                bring_h_diff(b, e)
+        for b in range(BATCH):
+            operand("hc_%d_1" % b, HALF_NODES)
+            for e in range(PAIR):
+                diffuse_beside(b, e)
         st_words = st_sb[:].bitcast(F32).rearrange("k (b p g) -> k b g p", b=BATCH, g=HALVES)
         st_bank = banks.tile([P, HALVES, BATCH, UNITS], F32, tag="bank")
         for g in range(HALVES):
@@ -210,9 +251,10 @@ def tile_gcrnncell_pb_s_kernel(tc, r_prev, h_diff, u, state, support0, support1,
             "p (g b k e) -> p g b e k", g=HALVES, b=BATCH, e=PAIR
         )
         for b in range(BATCH):
-            candidate_sums(b, 0)
-        for b in range(BATCH):
-            interleave(b, 1)
+            quantise("hc_%d_0" % b)
+            candidate_bank(b, 0)
+            for e in range(PAIR):
+                candidate_sums(b, 0, e)
         for g in range(HALVES):
             nc.vector.tensor_tensor(
                 out=kept[:, g],
@@ -221,6 +263,9 @@ def tile_gcrnncell_pb_s_kernel(tc, r_prev, h_diff, u, state, support0, support1,
                 op=ALU.mult,
             )
         for b in range(BATCH):
-            candidate_sums(b, 1)
+            candidate_bank(b, 1)
+            for e in range(PAIR):
+                quantise("hc_%d_1" % b, slice(e * P, (e + 1) * P))
+                candidate_sums(b, 1, e)
         for g in range(HALVES):
             blend(g)

@@ -24,7 +24,7 @@ PAIR = 2
 HALF_NODES = NODES // HALVES
 WORDS = NODES // 2
 
-WARM_PASSES = 9
+WARM_PASSES = 16
 
 FLOPS = 2 * BATCH * SUPPORTS * UNITS * NODES * NODES + 2 * BATCH * NODES * (FEATURES + SUPPORTS * UNITS) * UNITS
 
@@ -45,17 +45,17 @@ def tile_gcrnncell_pb_s_kernel(tc, r_prev, h_diff, u, state, support0, support1,
         nc.vector.memset(warm[:], 0.0)
         nc.scalar.activation(out=warm[:], in_=warm[:], func=ACT.Tanh)
 
-        idle_values = keep.tile([P, HALF_NODES * PACK], BF16, align_bytes=64)
-        idle_codes = keep.tile([P, HALF_NODES], U32, align_bytes=64)
-        idle_scales = keep.tile([P, HALF_NODES], U8, align_bytes=64)
+        idle_values = keep.tile([P, P * PACK], BF16, align_bytes=64)
+        idle_codes = keep.tile([P, P], U32, align_bytes=64)
+        idle_scales = keep.tile([P, P], U8, align_bytes=64)
         nc.vector.memset(idle_values[:].bitcast(I32), 0)
         nc.vector.quantize_mx(out=idle_codes[:].bitcast(FP8X4), scales=idle_scales[:], in_=idle_values[:])
-        idle_bank = banks.tile([P, HALF_NODES], F32, tag="bank")
+        idle_bank = banks.tile([P, P], F32, tag="bank")
         for k in range(WARM_PASSES):
             nc.tensor.matmul_mx(
                 out=idle_bank[:],
-                lhsT=idle_codes[:, 0:P].bitcast(FP8X4),
-                lhsT_scale=idle_scales[:, 0:P],
+                lhsT=idle_codes[:].bitcast(FP8X4),
+                lhsT_scale=idle_scales[:],
                 rhs=idle_codes[:].bitcast(FP8X4),
                 rhs_scale=idle_scales[:],
                 start=True,

@@ -24,7 +24,7 @@ PAIR = 2
 HALF_NODES = NODES // HALVES
 WORDS = NODES // 2
 
-WARM_PASSES = 16
+WARM_PASSES = 18
 
 FLOPS = 2 * BATCH * SUPPORTS * UNITS * NODES * NODES + 2 * BATCH * NODES * (FEATURES + SUPPORTS * UNITS) * UNITS
 
@@ -37,6 +37,8 @@ def tile_gcrnncell_pb_s_kernel(tc, r_prev, h_diff, u, state, support0, support1,
         banks = ctx.enter_context(tc.psum_pool(name="banks", bufs=8))
         ctx.enter_context(tc.manual_schedule())
 
+        idle_values = keep.tile([P, P * PACK], BF16, align_bytes=64)
+        nc.gpsimd.memset(idle_values[:].bitcast(I32), 0)
         ident = keep.tile([P, P], F32)
         make_identity(nc, ident[:])
         ident_bf = keep.tile([P, P], BF16)
@@ -45,10 +47,8 @@ def tile_gcrnncell_pb_s_kernel(tc, r_prev, h_diff, u, state, support0, support1,
         nc.vector.memset(warm[:], 0.0)
         nc.scalar.activation(out=warm[:], in_=warm[:], func=ACT.Tanh)
 
-        idle_values = keep.tile([P, P * PACK], BF16, align_bytes=64)
         idle_codes = keep.tile([P, P], U32, align_bytes=64)
         idle_scales = keep.tile([P, P], U8, align_bytes=64)
-        nc.vector.memset(idle_values[:].bitcast(I32), 0)
         nc.vector.quantize_mx(out=idle_codes[:].bitcast(FP8X4), scales=idle_scales[:], in_=idle_values[:])
         idle_bank = banks.tile([P, P], F32, tag="bank")
         for k in range(WARM_PASSES):
@@ -62,8 +62,8 @@ def tile_gcrnncell_pb_s_kernel(tc, r_prev, h_diff, u, state, support0, support1,
                 stop=True,
             )
 
-        r_sb = keep.tile([P, BATCH * NODES], BF16)
-        nc.sync.dma_start(out=r_sb[:].rearrange("k (b n) -> k b n", b=BATCH), in_=r_prev.rearrange("b k n -> k b n"))
+        r_sb = keep.tile([P, 2 * NODES], BF16)
+        nc.sync.dma_start(out=r_sb[:], in_=r_prev.rearrange("b (q s) n -> (b q) (s n)", s=2))
         sup_sb = {}
         for g in range(HALVES):
             for i in range(SUPPORTS):
@@ -108,13 +108,17 @@ def tile_gcrnncell_pb_s_kernel(tc, r_prev, h_diff, u, state, support0, support1,
                 out=codes[name][:, columns].bitcast(FP8X4), scales=scales[name][:, columns], in_=grouped[name][:, values]
             )
 
-        def flip(name, rows, engine):
+        def flip(name, rows, engine, alternate=False):
             operand(name, 2 * P)
-            bank = banks.tile([P, 2, 2 * P], F32, tag="bank", name="bank_%s" % name)
+            bank = banks.tile([P, 2, 2, P], F32, tag="bank", name="bank_%s" % name)
             for block in range(2):
                 for h in range(2):
-                    nc.tensor.transpose(bank[:, h, block * P : (block + 1) * P], rows[:, block, h * P : (h + 1) * P], ident[:])
-            copy(engine, grouped[name][:].bitcast(F32).rearrange("q (c h) -> q c h", h=2), bank[:].rearrange("q h c -> q c h"))
+                    nc.tensor.transpose(bank[:, h, block, :], rows[:, block, h * P : (h + 1) * P], ident[:])
+            words = grouped[name][:].bitcast(F32)
+            if alternate:
+                copy(engine, words.rearrange("q (x a h) -> q x a h", a=2, h=2), bank[:].rearrange("q h a x -> q x a h"))
+            else:
+                copy(engine, words.rearrange("q (a x h) -> q a x h", a=2, h=2), bank[:].rearrange("q h a x -> q a x h"))
 
         def flip_support(i, g, engine):
             flip("sup_%d_%d" % (i, g), sup_sb[i, g][:].bitcast(F32).rearrange("p (e w) -> p e w", e=PAIR), engine)
@@ -184,22 +188,21 @@ def tile_gcrnncell_pb_s_kernel(tc, r_prev, h_diff, u, state, support0, support1,
 
         c_bank = {}
 
-        def candidate_bank(b, g):
-            c_bank[b, g] = banks.tile([P, PAIR * UNITS], F32, tag="bank", name="c_bank_%d_%d" % (b, g))
-
-        def candidate_sums(b, g, e):
+        def candidate_sums(b, g):
             name = "hc_%d_%d" % (b, g)
-            nc.tensor.matmul_mx(
-                out=c_bank[b, g][:, e * UNITS : (e + 1) * UNITS],
-                lhsT=codes[name][:, e * P : (e + 1) * P].bitcast(FP8X4),
-                lhsT_scale=scales[name][:, e * P : (e + 1) * P],
-                rhs=codes["ck"][:].bitcast(FP8X4),
-                rhs_scale=scales["ck"][:],
-                start=True,
-                stop=True,
-            )
+            c_bank[b, g] = banks.tile([P, PAIR * UNITS], F32, tag="bank", name="c_bank_%d_%d" % (b, g))
+            for e in range(PAIR):
+                nc.tensor.matmul_mx(
+                    out=c_bank[b, g][:, e * UNITS : (e + 1) * UNITS],
+                    lhsT=codes[name][:, e * P : (e + 1) * P].bitcast(FP8X4),
+                    lhsT_scale=scales[name][:, e * P : (e + 1) * P],
+                    rhs=codes["ck"][:].bitcast(FP8X4),
+                    rhs_scale=scales["ck"][:],
+                    start=True,
+                    stop=True,
+                )
 
-        kept = keep.tile([P, HALVES, BATCH, PAIR, UNITS], F32)
+        kept = keep.tile([P, BATCH, HALVES, PAIR, UNITS], F32)
         out_view = out.rearrange("b (p g x) -> b g p x", p=P, g=HALVES)
 
         def blend(g):
@@ -214,11 +217,11 @@ def tile_gcrnncell_pb_s_kernel(tc, r_prev, h_diff, u, state, support0, support1,
                 )
             for b in range(BATCH):
                 nc.vector.tensor_tensor(
-                    out=z[b][:], in0=kept[:, g, b].rearrange("p e k -> p (e k)"), in1=minus[b][:], op=ALU.subtract
+                    out=z[b][:], in0=kept[:, b, g].rearrange("p e k -> p (e k)"), in1=minus[b][:], op=ALU.subtract
                 )
                 nc.sync.dma_start(out=out_view[b, g], in_=z[b][:])
 
-        flip("r", r_sb[:].bitcast(F32).rearrange("k (b w) -> k b w", b=BATCH), "scalar")
+        flip("r", r_sb[:].bitcast(F32).rearrange("p (s w) -> p s w", s=2), "scalar", alternate=True)
         flip_support(0, 0, "vector")
         quantise("r")
         quantise("sup_0_0")
@@ -243,29 +246,21 @@ def tile_gcrnncell_pb_s_kernel(tc, r_prev, h_diff, u, state, support0, support1,
             for e in range(PAIR):
                 diffuse_beside(b, e)
         st_words = st_sb[:].bitcast(F32).rearrange("k (b p g) -> k b g p", b=BATCH, g=HALVES)
-        st_bank = banks.tile([P, HALVES, BATCH, UNITS], F32, tag="bank")
-        for g in range(HALVES):
-            for b in range(BATCH):
-                nc.tensor.transpose(st_bank[:, g, b, :], st_words[:, b, g, :], ident[:])
-        prev_t = st_bank[:].rearrange("p g b k -> p (g b k)").bitcast(BF16).rearrange(
-            "p (g b k e) -> p g b e k", g=HALVES, b=BATCH, e=PAIR
-        )
+        st_bank = banks.tile([P, BATCH, HALVES, UNITS], F32, tag="bank")
+        for b in range(BATCH):
+            for g in range(HALVES):
+                nc.tensor.transpose(st_bank[:, b, g, :], st_words[:, b, g, :], ident[:])
         for b in range(BATCH):
             quantise("hc_%d_0" % b)
-            candidate_bank(b, 0)
-            for e in range(PAIR):
-                candidate_sums(b, 0, e)
-        for g in range(HALVES):
-            nc.vector.tensor_tensor(
-                out=kept[:, g],
-                in0=u_sb[:, :, g, :].rearrange("p b (e k) -> p b e k", e=PAIR),
-                in1=prev_t[:, g],
-                op=ALU.mult,
-            )
+            candidate_sums(b, 0)
+        nc.vector.tensor_tensor(
+            out=kept[:].rearrange("p b g e k -> p (b g) e k"),
+            in0=u_sb[:].rearrange("p b g (e k) -> p (b g) e k", e=PAIR),
+            in1=st_bank[:].rearrange("p b g k -> p (b g k)").bitcast(BF16).rearrange("p (x k e) -> p x e k", k=UNITS, e=PAIR),
+            op=ALU.mult,
+        )
         for b in range(BATCH):
-            candidate_bank(b, 1)
-            for e in range(PAIR):
-                quantise("hc_%d_1" % b, slice(e * P, (e + 1) * P))
-                candidate_sums(b, 1, e)
+            quantise("hc_%d_1" % b)
+            candidate_sums(b, 1)
         for g in range(HALVES):
             blend(g)

@@ -231,7 +231,7 @@ def tile_gcrnncell_pb_s_kernel(tc, r_prev, h_diff, u, state, support0, support1,
             flip_support(i, 1, "scalar")
             quantise("sup_%d_1" % i)
         operand("ck", UNITS)
-        nc.vector.tensor_copy(out=grouped["ck"][:].rearrange("q (k t) -> q k t", t=PACK), in_=ck_sb[:].rearrange("q t k -> q k t"))
+        nc.gpsimd.tensor_copy(out=grouped["ck"][:].rearrange("q (k t) -> q k t", t=PACK), in_=ck_sb[:].rearrange("q t k -> q k t"))
         for b in range(BATCH):
             flip_h_diff(b)
             diffuse(b)

from contextlib import ExitStack

import concourse.mybir as mybir
from concourse.masks import make_identity

F32 = mybir.dt.float32
BF16 = mybir.dt.bfloat16
U32 = mybir.dt.uint32
U8 = mybir.dt.uint8
I32 = mybir.dt.int32
FP8X4 = mybir.dt.float8_e4m3fn_x4
ACT = mybir.ActivationFunctionType
ALU = mybir.AluOpType

P = 128
PACK = 4
BATCH = 2
NODES = 512
UNITS = 128
SUPPORTS = 2
FEATURES = 256
HALVES = 2
PAIR = 2
HALF_NODES = NODES // HALVES
WORDS = NODES // 2

WARM_PASSES = 18

FLOPS = 2 * BATCH * SUPPORTS * UNITS * NODES * NODES + 2 * BATCH * NODES * (FEATURES + SUPPORTS * UNITS) * UNITS


def tile_gcrnncell_pb_s_kernel(tc, r_prev, h_diff, u, state, support0, support1, c_kernel, out):
    nc = tc.nc
    supports = (support0, support1)
    with ExitStack() as ctx:
        keep = ctx.enter_context(tc.tile_pool(name="keep", bufs=1))
        banks = ctx.enter_context(tc.psum_pool(name="banks", bufs=8))
        ctx.enter_context(tc.manual_schedule())

        idle_values = keep.tile([P, P * PACK], BF16, align_bytes=64)
        nc.gpsimd.memset(idle_values[:].bitcast(I32), 0)
        ident = keep.tile([P, P], F32)
        make_identity(nc, ident[:])
        ident_bf = keep.tile([P, P], BF16)
        make_identity(nc, ident_bf[:])
        warm = keep.tile([P, 1], F32)
        nc.vector.memset(warm[:], 0.0)
        nc.scalar.activation(out=warm[:], in_=warm[:], func=ACT.Tanh)

        idle_codes = keep.tile([P, P], U32, align_bytes=64)
        idle_scales = keep.tile([P, P], U8, align_bytes=64)
        nc.vector.quantize_mx(out=idle_codes[:].bitcast(FP8X4), scales=idle_scales[:], in_=idle_values[:])
        idle_bank = banks.tile([P, P], F32, tag="bank")
        for k in range(WARM_PASSES):
            nc.tensor.matmul_mx(
                out=idle_bank[:],
                lhsT=idle_codes[:].bitcast(FP8X4),
                lhsT_scale=idle_scales[:],
                rhs=idle_codes[:].bitcast(FP8X4),
                rhs_scale=idle_scales[:],
                start=True,
                stop=True,
            )

        r_sb = keep.tile([P, 2 * NODES], BF16)
        nc.sync.dma_start(out=r_sb[:], in_=r_prev.rearrange("b (q s) n -> (b q) (s n)", s=2))
        sup_sb = {}
        for g in range(HALVES):
            for i in range(SUPPORTS):
                sup_sb[i, g] = keep.tile([P, PAIR * NODES], BF16, name="sup_sb_%d_%d" % (i, g))
                nc.sync.dma_start(
                    out=sup_sb[i, g][:],
                    in_=supports[i].rearrange("(p g e) n -> g p (e n)", g=HALVES, e=PAIR)[g],
                )
        hd_sb = []
        for b in range(BATCH):
            hd_sb.append(keep.tile([P, NODES // P * FEATURES], BF16, name="hd_sb_%d" % b))
            nc.sync.dma_start(out=hd_sb[b][:], in_=h_diff[b].rearrange("(p j) c -> p (j c)", p=P))
        ck_sb = keep.tile([P, PACK, UNITS], BF16)
        nc.sync.dma_start(out=ck_sb[:, 0:2, :], in_=c_kernel[0:FEATURES, :].rearrange("(q s) k -> q s k", s=2))
        nc.sync.dma_start(out=ck_sb[:, 2:4, :], in_=c_kernel[FEATURES:, :].rearrange("(i q) k -> q i k", q=P))
        st_sb = keep.tile([P, BATCH * NODES], BF16)
        nc.sync.dma_start(out=st_sb[:].rearrange("k (b n) -> k b n", b=BATCH), in_=state.rearrange("b (k n) -> k b n", n=NODES))
        u_sb = keep.tile([P, BATCH, HALVES, PAIR * UNITS], BF16)
        nc.sync.dma_start(
            out=u_sb[:].rearrange("p b g x -> p b (g x)"),
            in_=u.rearrange("b (p j) k -> p b (j k)", p=P),
        )

        def copy(engine, out_ap, in_ap):
            if engine == "vector":
                nc.vector.tensor_copy(out=out_ap, in_=in_ap)
            else:
                nc.scalar.copy(out=out_ap, in_=in_ap)

        grouped = {}
        codes = {}
        scales = {}

        def operand(name, columns):
            grouped[name] = keep.tile([P, columns * PACK], BF16, name="grouped_%s" % name, align_bytes=64)
            codes[name] = keep.tile([P, columns], U32, name="codes_%s" % name, align_bytes=64)
            scales[name] = keep.tile([P, columns], U8, name="scales_%s" % name, align_bytes=64)

        def quantise(name, columns=slice(0, 2 * P)):
            values = slice(columns.start * PACK, columns.stop * PACK)
            nc.vector.quantize_mx(
                out=codes[name][:, columns].bitcast(FP8X4), scales=scales[name][:, columns], in_=grouped[name][:, values]
            )

        def flip(name, rows, engine, alternate=False):
            operand(name, 2 * P)
            bank = banks.tile([P, 2, 2, P], F32, tag="bank", name="bank_%s" % name)
            for block in range(2):
                for h in range(2):
                    nc.tensor.transpose(bank[:, h, block, :], rows[:, block, h * P : (h + 1) * P], ident[:])
            words = grouped[name][:].bitcast(F32)
            if alternate:
                copy(engine, words.rearrange("q (x a h) -> q x a h", a=2, h=2), bank[:].rearrange("q h a x -> q x a h"))
            else:
                copy(engine, words.rearrange("q (a x h) -> q a x h", a=2, h=2), bank[:].rearrange("q h a x -> q a x h"))

        def flip_support(i, g, engine):
            flip("sup_%d_%d" % (i, g), sup_sb[i, g][:].bitcast(F32).rearrange("p (e w) -> p e w", e=PAIR), engine)

        planes = [keep.tile([P, 2, HALF_NODES], F32, name="planes_%d" % b) for b in range(BATCH)]

        def flip_h_diff(b):
            hd_words = hd_sb[b][:].bitcast(F32).rearrange("p (j w) -> p j w", w=FEATURES // 2)
            h_bank = banks.tile([P, HALF_NODES], F32, tag="bank")
            for j in range(PAIR):
                nc.tensor.transpose(h_bank[:, j * P : (j + 1) * P], hd_words[:, j, :], ident[:])
            copy(("scalar", "vector")[b], planes[b][:, 0, :], h_bank[:])

        def diffuse(b):
            d_bank = banks.tile([P, SUPPORTS, HALF_NODES], F32, tag="bank")
            for i in range(SUPPORTS):
                nc.tensor.matmul_mx(
                    out=d_bank[:, i, :],
                    lhsT=codes["r"][:, b * UNITS : (b + 1) * UNITS].bitcast(FP8X4),
                    lhsT_scale=scales["r"][:, b * UNITS : (b + 1) * UNITS],
                    rhs=codes["sup_%d_0" % i][:].bitcast(FP8X4),
                    rhs_scale=scales["sup_%d_0" % i][:],
                    start=True,
                    stop=True,
                )
            copy(
                "scalar",
                planes[b][:, 1, :].bitcast(BF16).rearrange("q (c i) -> q c i", i=SUPPORTS),
                d_bank[:].rearrange("q i c -> q c i"),
            )

        def interleave(b):
            name = "hc_%d_0" % b
            operand(name, HALF_NODES)
            nc.vector.tensor_copy(
                out=grouped[name][:].bitcast(F32).rearrange("q (c w) -> q c w", w=2),
                in_=planes[b][:].rearrange("q w c -> q c w"),
            )

        hc_bank = {}

        def bring_h_diff(b, e):
            hc_bank[b, e] = banks.tile([P, PACK, P], F32, tag="bank", name="hc_bank_%d_%d" % (b, e))
            first = (PAIR + e) * FEATURES
            for s in range(2):
                nc.tensor.matmul(
                    out=hc_bank[b, e][:, s, :], lhsT=hd_sb[b][:, first + s : first + FEATURES : 2], rhs=ident_bf[:], start=True, stop=True
                )

        def diffuse_beside(b, e):
            for i in range(SUPPORTS):
                name = "sup_%d_1" % i
                nc.tensor.matmul_mx(
                    out=hc_bank[b, e][:, SUPPORTS + i, :],
                    lhsT=codes["r"][:, b * UNITS : (b + 1) * UNITS].bitcast(FP8X4),
                    lhsT_scale=scales["r"][:, b * UNITS : (b + 1) * UNITS],
                    rhs=codes[name][:, e * P : (e + 1) * P].bitcast(FP8X4),
                    rhs_scale=scales[name][:, e * P : (e + 1) * P],
                    start=True,
                    stop=True,
                )
            copy(
                "scalar",
                grouped["hc_%d_1" % b][:, e * P * PACK : (e + 1) * P * PACK].rearrange("q (c t) -> q c t", t=PACK),
                hc_bank[b, e][:].rearrange("q t c -> q c t"),
            )

        c_bank = {}

        def candidate_sums(b, g):
            name = "hc_%d_%d" % (b, g)
            c_bank[b, g] = banks.tile([P, PAIR * UNITS], F32, tag="bank", name="c_bank_%d_%d" % (b, g))
            for e in range(PAIR):
                nc.tensor.matmul_mx(
                    out=c_bank[b, g][:, e * UNITS : (e + 1) * UNITS],
                    lhsT=codes[name][:, e * P : (e + 1) * P].bitcast(FP8X4),
                    lhsT_scale=scales[name][:, e * P : (e + 1) * P],
                    rhs=codes["ck"][:].bitcast(FP8X4),
                    rhs_scale=scales["ck"][:],
                    start=True,
                    stop=True,
                )

        kept = keep.tile([P, BATCH, HALVES, PAIR, UNITS], F32)
        out_view = out.rearrange("b (p g x) -> b g p x", p=P, g=HALVES)

        def blend(g):
            cand = [keep.tile([P, PAIR * UNITS], F32, name="cand_%d_%d" % (b, g)) for b in range(BATCH)]
            minus = [keep.tile([P, PAIR * UNITS], F32, name="minus_%d_%d" % (b, g)) for b in range(BATCH)]
            z = [keep.tile([P, PAIR * UNITS], F32, name="z_%d_%d" % (b, g)) for b in range(BATCH)]
            for b in range(BATCH):
                nc.scalar.activation(out=cand[b][:], in_=c_bank[b, g][:], func=ACT.Tanh)
            for b in range(BATCH):
                nc.vector.scalar_tensor_tensor(
                    out=minus[b][:], in0=u_sb[:, b, g, :], scalar=1.0, in1=cand[b][:], op0=ALU.subtract, op1=ALU.mult
                )
            for b in range(BATCH):
                nc.vector.tensor_tensor(
                    out=z[b][:], in0=kept[:, b, g].rearrange("p e k -> p (e k)"), in1=minus[b][:], op=ALU.subtract
                )
                nc.sync.dma_start(out=out_view[b, g], in_=z[b][:])

        flip("r", r_sb[:].bitcast(F32).rearrange("p (s w) -> p s w", s=2), "scalar", alternate=True)
        flip_support(0, 0, "vector")
        quantise("r")
        quantise("sup_0_0")
        flip_support(1, 0, "scalar")
        quantise("sup_1_0")
        for i in range(SUPPORTS):
            flip_support(i, 1, "scalar")
            quantise("sup_%d_1" % i)
        operand("ck", UNITS)
        nc.gpsimd.tensor_copy(out=grouped["ck"][:].rearrange("q (k t) -> q k t", t=PACK), in_=ck_sb[:].rearrange("q t k -> q k t"))
        for b in range(BATCH):
            flip_h_diff(b)
            diffuse(b)
        interleave(0)
        quantise("ck", slice(0, UNITS))
        interleave(1)
        for b in range(BATCH):
            for e in range(PAIR):
                bring_h_diff(b, e)
        for b in range(BATCH):
            operand("hc_%d_1" % b, HALF_NODES)
            for e in range(PAIR):
                diffuse_beside(b, e)
        st_words = st_sb[:].bitcast(F32).rearrange("k (b p g) -> k b g p", b=BATCH, g=HALVES)
        st_bank = banks.tile([P, BATCH, HALVES, UNITS], F32, tag="bank")
        for b in range(BATCH):
            for g in range(HALVES):
                nc.tensor.transpose(st_bank[:, b, g, :], st_words[:, b, g, :], ident[:])
        for b in range(BATCH):
            quantise("hc_%d_0" % b)
            candidate_sums(b, 0)
        nc.vector.tensor_tensor(
            out=kept[:].rearrange("p b g e k -> p (b g) e k"),
            in0=u_sb[:].rearrange("p b g (e k) -> p (b g) e k", e=PAIR),
            in1=st_bank[:].rearrange("p b g k -> p (b g k)").bitcast(BF16).rearrange("p (x k e) -> p x e k", k=UNITS, e=PAIR),
            op=ALU.mult,
        )
        for b in range(BATCH):
            quantise("hc_%d_1" % b)
            candidate_sums(b, 1)
        for g in range(HALVES):
            blend(g)
